import numpy as np
import ml_dtypes

BF16 = ml_dtypes.bfloat16


def bf(x):
    return np.asarray(x, np.float32).astype(BF16)


def f32(x):
    return np.asarray(x, np.float32)


def f64(x):
    return np.asarray(x).astype(np.float64)


def striped(idx):
    return np.tile(idx.reshape(-1, 16).T, (8, 1))


A, T, C, S, N, D = 2, 512, 1024, 384, 128, 256
MIN = 2.0 ** -14
EPS = MIN * (1.0 + MIN) ** 2


def setup_inputs():
    return {"x": f32(np.random.random((C, S)) ** 8), "other": f32(np.random.random((C, N)) ** 8), "context": bf(np.random.standard_normal((T, D))), "offs": striped(np.random.permutation(np.tile(np.arange(S), 2))[:N])}


def reference(x, other, context, offs):
    idx = offs[:16].T.reshape(-1)
    q = (f64(x)[:, idx] * f64(other)).reshape(A, T, N).sum(axis=0)
    return (f64(context).T @ q) / (q.sum(axis=0, keepdims=True) + EPS)

@@ -1,0 +1,81 @@
+import concourse.mybir as mybir
+
+F32, BF16, U16 = mybir.dt.float32, mybir.dt.bfloat16, mybir.dt.uint16
+MULT, ADD = mybir.AluOpType.mult, mybir.AluOpType.add
+
+P = 128
+HEADS = 2
+TOKENS = 512
+ENTITIES = 384
+PAIRS = 128
+FEATURES = 256
+TOKEN_BLOCKS = TOKENS // P
+FEATURE_BLOCKS = FEATURES // P
+EPS = 2.0**-14 * (1.0 + 2.0**-14) ** 2
+
+FLOPS = 2 * HEADS * TOKENS * PAIRS + 2 * TOKENS * PAIRS * (FEATURES + 1)
+
+
+def tile_remodel_kernel(tc, x, other, context, offs, out):
+    nc = tc.nc
+
+    x_blocks = x.rearrange("(a p k) s -> a k p s", a=HEADS, p=P, k=TOKEN_BLOCKS)
+    other_heads = other.rearrange("(a p k) j -> a p (k j)", a=HEADS, p=P, k=TOKEN_BLOCKS)
+    context_rows = context.rearrange("(p k) d -> p (k d)", p=P, k=TOKEN_BLOCKS)
+    out_blocks = out.rearrange("(b p) j -> b p j", p=P)
+
+    with (
+        tc.tile_pool(name="held", bufs=1) as held,
+        tc.psum_pool(name="psum", bufs=1) as psum,
+    ):
+        offsets = held.tile([P, PAIRS // 16], U16, name="offsets")
+        nc.sync.dma_start(offsets[:], offs)
+
+        queues = (nc.sync, nc.scalar)
+        other_tiles = []
+        for a in range(HEADS):
+            other_tile = held.tile([P, TOKEN_BLOCKS * PAIRS], F32, name=f"other{a}")
+            queues[a].dma_start(other_tile[:], other_heads[a])
+            other_tiles.append(other_tile)
+        context_tile = held.tile([P, TOKEN_BLOCKS * FEATURES], BF16, name="context_tile")
+        nc.gpsimd.dma_start(context_tile[:], context_rows)
+        windows = {}
+        for k in range(TOKEN_BLOCKS):
+            for a in range(HEADS):
+                windows[a, k] = held.tile([P, ENTITIES], F32, name=f"window{a}_{k}")
+                queues[a].dma_start(windows[a, k][:], x_blocks[a, k])
+
+        ones = held.tile([P, P], BF16, name="ones")
+        nc.gpsimd.memset(ones[:], 1.0)
+
+        numerators = [psum.tile([P, PAIRS], F32, name=f"numerator{b}") for b in range(FEATURE_BLOCKS)]
+        denominator = psum.tile([P, PAIRS], F32, name="denominator")
+
+        for k in range(TOKEN_BLOCKS):
+            products = []
+            for a in range(HEADS):
+                product = held.tile([P, PAIRS], F32, name=f"product{a}_{k}")
+                nc.vector.tensor_tensor(
+                    product[:],
+                    windows[a, k][:].indirect(offsets[:]),
+                    other_tiles[a][:, k * PAIRS : (k + 1) * PAIRS],
+                    MULT,
+                )
+                products.append(product)
+            q = held.tile([P, PAIRS], BF16, name=f"q{k}")
+            nc.vector.tensor_tensor(q[:], products[0][:], products[1][:], ADD)
+
+            first, last = k == 0, k == TOKEN_BLOCKS - 1
+            nc.tensor.matmul(denominator[:], ones[:], q[:], start=first, stop=last)
+            for b in range(FEATURE_BLOCKS):
+                features = context_tile[:, k * FEATURES + b * P : k * FEATURES + (b + 1) * P]
+                nc.tensor.matmul(numerators[b][:], features, q[:], start=first, stop=last)
+
+        shifted = held.tile([P, PAIRS], F32, name="shifted")
+        nc.vector.tensor_scalar_add(shifted[:], denominator[:], EPS)
+        inverse = held.tile([P, PAIRS], F32, name="inverse")
+        nc.vector.reciprocal(inverse[:], shifted[:])
+        for b in range(FEATURE_BLOCKS):
+            pooled = held.tile([P, PAIRS], F32, name=f"pooled{b}")
+            nc.vector.tensor_tensor(pooled[:], numerators[b][:], inverse[:], MULT)
+            queues[b].dma_start(out_blocks[b], pooled[:])

@@ -37,20 +37,19 @@ def tile_remodel_kernel(tc, x, other, context, offs, out):
             other_tile = held.tile([P, TOKEN_BLOCKS * PAIRS], F32, name=f"other{a}")
             queues[a].dma_start(other_tile[:], other_heads[a])
             other_tiles.append(other_tile)
-        context_tile = held.tile([P, TOKEN_BLOCKS * FEATURES], BF16, name="context_tile")
-        nc.gpsimd.dma_start(context_tile[:], context_rows)
         windows = {}
         for k in range(TOKEN_BLOCKS):
             for a in range(HEADS):
                 windows[a, k] = held.tile([P, ENTITIES], F32, name=f"window{a}_{k}")
                 queues[a].dma_start(windows[a, k][:], x_blocks[a, k])
+        context_tile = held.tile([P, TOKEN_BLOCKS * FEATURES], BF16, name="context_tile")
+        nc.scalar.dma_start(context_tile[:], context_rows)
 
         ones = held.tile([P, P], BF16, name="ones")
         nc.gpsimd.memset(ones[:], 1.0)
 
-        numerators = [psum.tile([P, PAIRS], F32, name=f"numerator{b}") for b in range(FEATURE_BLOCKS)]
         denominator = psum.tile([P, PAIRS], F32, name="denominator")
-
+        q_blocks = []
         for k in range(TOKEN_BLOCKS):
             products = []
             for a in range(HEADS):
@@ -64,18 +63,19 @@ def tile_remodel_kernel(tc, x, other, context, offs, out):
                 products.append(product)
             q = held.tile([P, PAIRS], BF16, name=f"q{k}")
             nc.vector.tensor_tensor(q[:], products[0][:], products[1][:], ADD)
-
-            first, last = k == 0, k == TOKEN_BLOCKS - 1
-            nc.tensor.matmul(denominator[:], ones[:], q[:], start=first, stop=last)
-            for b in range(FEATURE_BLOCKS):
-                features = context_tile[:, k * FEATURES + b * P : k * FEATURES + (b + 1) * P]
-                nc.tensor.matmul(numerators[b][:], features, q[:], start=first, stop=last)
+            nc.tensor.matmul(denominator[:], ones[:], q[:], start=k == 0, stop=k == TOKEN_BLOCKS - 1)
+            q_blocks.append(q)
 
         shifted = held.tile([P, PAIRS], F32, name="shifted")
         nc.vector.tensor_scalar_add(shifted[:], denominator[:], EPS)
         inverse = held.tile([P, PAIRS], F32, name="inverse")
         nc.vector.reciprocal(inverse[:], shifted[:])
+
         for b in range(FEATURE_BLOCKS):
+            numerator = psum.tile([P, PAIRS], F32, name=f"numerator{b}")
+            for k in range(TOKEN_BLOCKS):
+                features = context_tile[:, k * FEATURES + b * P : k * FEATURES + (b + 1) * P]
+                nc.tensor.matmul(numerator[:], features, q_blocks[k][:], start=k == 0, stop=k == TOKEN_BLOCKS - 1)
             pooled = held.tile([P, PAIRS], F32, name=f"pooled{b}")
-            nc.vector.tensor_tensor(pooled[:], numerators[b][:], inverse[:], MULT)
+            nc.vector.tensor_tensor(pooled[:], numerator[:], inverse[:], MULT)
             queues[b].dma_start(out_blocks[b], pooled[:])

@@ -31,19 +31,18 @@ def tile_remodel_kernel(tc, x, other, context, offs, out):
         offsets = held.tile([P, PAIRS // 16], U16, name="offsets")
         nc.sync.dma_start(offsets[:], offs)
 
-        queues = (nc.sync, nc.scalar)
         other_tiles = []
         for a in range(HEADS):
             other_tile = held.tile([P, TOKEN_BLOCKS * PAIRS], F32, name=f"other{a}")
-            queues[a].dma_start(other_tile[:], other_heads[a])
+            nc.sync.dma_start(other_tile[:], other_heads[a])
             other_tiles.append(other_tile)
         windows = {}
         for k in range(TOKEN_BLOCKS):
             for a in range(HEADS):
                 windows[a, k] = held.tile([P, ENTITIES], F32, name=f"window{a}_{k}")
-                queues[a].dma_start(windows[a, k][:], x_blocks[a, k])
+                nc.sync.dma_start(windows[a, k][:], x_blocks[a, k])
         context_tile = held.tile([P, TOKEN_BLOCKS * FEATURES], BF16, name="context_tile")
-        nc.scalar.dma_start(context_tile[:], context_rows)
+        nc.sync.dma_start(context_tile[:], context_rows)
 
         ones = held.tile([P, P], BF16, name="ones")
         nc.gpsimd.memset(ones[:], 1.0)
@@ -71,6 +70,7 @@ def tile_remodel_kernel(tc, x, other, context, offs, out):
         inverse = held.tile([P, PAIRS], F32, name="inverse")
         nc.vector.reciprocal(inverse[:], shifted[:])
 
+        store_queues = (nc.sync, nc.scalar)
         for b in range(FEATURE_BLOCKS):
             numerator = psum.tile([P, PAIRS], F32, name=f"numerator{b}")
             for k in range(TOKEN_BLOCKS):
@@ -78,4 +78,4 @@ def tile_remodel_kernel(tc, x, other, context, offs, out):
                 nc.tensor.matmul(numerator[:], features, q_blocks[k][:], start=k == 0, stop=k == TOKEN_BLOCKS - 1)
             pooled = held.tile([P, PAIRS], F32, name=f"pooled{b}")
             nc.vector.tensor_tensor(pooled[:], numerator[:], inverse[:], MULT)
-            queues[b].dma_start(out_blocks[b], pooled[:])
+            store_queues[b].dma_start(out_blocks[b], pooled[:])

@@ -47,7 +47,12 @@ def tile_remodel_kernel(tc, x, other, context, offs, out):
         ones = held.tile([P, P], BF16, name="ones")
         nc.gpsimd.memset(ones[:], 1.0)
 
+        ones_f32 = held.tile([P, P], F32, name="ones_f32")
+        nc.gpsimd.memset(ones_f32[:], 1.0)
+        eps_share = held.tile([P, PAIRS], F32, name="eps_share")
+        nc.gpsimd.memset(eps_share[:], EPS / P)
         denominator = psum.tile([P, PAIRS], F32, name="denominator")
+        nc.tensor.matmul(denominator[:], ones_f32[:], eps_share[:], start=True, stop=False)
         q_blocks = []
         for k in range(TOKEN_BLOCKS):
             products = []
@@ -62,13 +67,11 @@ def tile_remodel_kernel(tc, x, other, context, offs, out):
                 products.append(product)
             q = held.tile([P, PAIRS], BF16, name=f"q{k}")
             nc.vector.tensor_tensor(q[:], products[0][:], products[1][:], ADD)
-            nc.tensor.matmul(denominator[:], ones[:], q[:], start=k == 0, stop=k == TOKEN_BLOCKS - 1)
+            nc.tensor.matmul(denominator[:], ones[:], q[:], start=False, stop=k == TOKEN_BLOCKS - 1)
             q_blocks.append(q)
 
-        shifted = held.tile([P, PAIRS], F32, name="shifted")
-        nc.vector.tensor_scalar_add(shifted[:], denominator[:], EPS)
         inverse = held.tile([P, PAIRS], F32, name="inverse")
-        nc.vector.reciprocal(inverse[:], shifted[:])
+        nc.vector.reciprocal(inverse[:], denominator[:])
 
         store_queues = (nc.sync, nc.scalar)
         for b in range(FEATURE_BLOCKS):

@@ -22,7 +22,7 @@ def tile_remodel_kernel(tc, x, other, context, offs, out):
     x_blocks = x.rearrange("(a p k) s -> a k p s", a=HEADS, p=P, k=TOKEN_BLOCKS)
     other_heads = other.rearrange("(a p k) j -> a p (k j)", a=HEADS, p=P, k=TOKEN_BLOCKS)
     context_rows = context.rearrange("(p k) d -> p (k d)", p=P, k=TOKEN_BLOCKS)
-    out_blocks = out.rearrange("(b p) j -> b p j", p=P)
+    out_rows = out.rearrange("(b p) j -> p b j", p=P)
 
     with (
         tc.tile_pool(name="held", bufs=1) as held,
@@ -73,12 +73,12 @@ def tile_remodel_kernel(tc, x, other, context, offs, out):
         inverse = held.tile([P, PAIRS], F32, name="inverse")
         nc.vector.reciprocal(inverse[:], denominator[:])
 
-        store_queues = (nc.sync, nc.scalar)
+        numerators = psum.tile([P, FEATURE_BLOCKS, PAIRS], F32, name="numerators")
         for b in range(FEATURE_BLOCKS):
-            numerator = psum.tile([P, PAIRS], F32, name=f"numerator{b}")
             for k in range(TOKEN_BLOCKS):
                 features = context_tile[:, k * FEATURES + b * P : k * FEATURES + (b + 1) * P]
-                nc.tensor.matmul(numerator[:], features, q_blocks[k][:], start=k == 0, stop=k == TOKEN_BLOCKS - 1)
-            pooled = held.tile([P, PAIRS], F32, name=f"pooled{b}")
-            nc.vector.tensor_tensor(pooled[:], numerator[:], inverse[:], MULT)
-            store_queues[b].dma_start(out_blocks[b], pooled[:])
+                nc.tensor.matmul(numerators[:, b, :], features, q_blocks[k][:], start=k == 0, stop=k == TOKEN_BLOCKS - 1)
+        pooled = held.tile([P, FEATURE_BLOCKS, PAIRS], F32, name="pooled")
+        inverse_for_each_block = inverse[:].unsqueeze(1).to_broadcast([P, FEATURE_BLOCKS, PAIRS])
+        nc.vector.tensor_tensor(pooled[:], numerators[:], inverse_for_each_block, MULT)
+        nc.sync.dma_start(out_rows, pooled[:])

@@ -34,15 +34,15 @@ def tile_remodel_kernel(tc, x, other, context, offs, out):
         other_tiles = []
         for a in range(HEADS):
             other_tile = held.tile([P, TOKEN_BLOCKS * PAIRS], F32, name=f"other{a}")
-            nc.sync.dma_start(other_tile[:], other_heads[a])
+            nc.scalar.dma_start(other_tile[:], other_heads[a])
             other_tiles.append(other_tile)
         windows = {}
         for k in range(TOKEN_BLOCKS):
             for a in range(HEADS):
                 windows[a, k] = held.tile([P, ENTITIES], F32, name=f"window{a}_{k}")
-                nc.sync.dma_start(windows[a, k][:], x_blocks[a, k])
+                nc.scalar.dma_start(windows[a, k][:], x_blocks[a, k])
         context_tile = held.tile([P, TOKEN_BLOCKS * FEATURES], BF16, name="context_tile")
-        nc.sync.dma_start(context_tile[:], context_rows)
+        nc.scalar.dma_start(context_tile[:], context_rows)
 
         ones = held.tile([P, P], BF16, name="ones")
         nc.gpsimd.memset(ones[:], 1.0)

@@ -31,18 +31,17 @@ def tile_remodel_kernel(tc, x, other, context, offs, out):
         offsets = held.tile([P, PAIRS // 16], U16, name="offsets")
         nc.sync.dma_start(offsets[:], offs)
 
-        other_tiles = []
-        for a in range(HEADS):
-            other_tile = held.tile([P, TOKEN_BLOCKS * PAIRS], F32, name=f"other{a}")
-            nc.scalar.dma_start(other_tile[:], other_heads[a])
-            other_tiles.append(other_tile)
+        other_tiles = {}
         windows = {}
         for k in range(TOKEN_BLOCKS):
             for a in range(HEADS):
+                if k == 0:
+                    other_tiles[a] = held.tile([P, TOKEN_BLOCKS * PAIRS], F32, name=f"other{a}")
+                    nc.sync.dma_start(other_tiles[a][:], other_heads[a])
                 windows[a, k] = held.tile([P, ENTITIES], F32, name=f"window{a}_{k}")
-                nc.scalar.dma_start(windows[a, k][:], x_blocks[a, k])
+                nc.sync.dma_start(windows[a, k][:], x_blocks[a, k])
         context_tile = held.tile([P, TOKEN_BLOCKS * FEATURES], BF16, name="context_tile")
-        nc.scalar.dma_start(context_tile[:], context_rows)
+        nc.sync.dma_start(context_tile[:], context_rows)
 
         ones = held.tile([P, P], BF16, name="ones")
         nc.gpsimd.memset(ones[:], 1.0)

@@ -37,7 +37,7 @@ def tile_remodel_kernel(tc, x, other, context, offs, out):
             for a in range(HEADS):
                 if k == 0:
                     other_tiles[a] = held.tile([P, TOKEN_BLOCKS * PAIRS], F32, name=f"other{a}")
-                    nc.sync.dma_start(other_tiles[a][:], other_heads[a])
+                    nc.scalar.dma_start(other_tiles[a][:], other_heads[a])
                 windows[a, k] = held.tile([P, ENTITIES], F32, name=f"window{a}_{k}")
                 nc.sync.dma_start(windows[a, k][:], x_blocks[a, k])
         context_tile = held.tile([P, TOKEN_BLOCKS * FEATURES], BF16, name="context_tile")

@@ -15,13 +15,16 @@ EPS = 2.0**-14 * (1.0 + 2.0**-14) ** 2
 
 FLOPS = 2 * HEADS * TOKENS * PAIRS + 2 * TOKENS * PAIRS * (FEATURES + 1)
 
+CONTEXT_PARTS = 2
+BLOCKS_IN_PART = TOKEN_BLOCKS // CONTEXT_PARTS
+
 
 def tile_remodel_kernel(tc, x, other, context, offs, out):
     nc = tc.nc
 
     x_blocks = x.rearrange("(a p k) s -> a k p s", a=HEADS, p=P, k=TOKEN_BLOCKS)
     other_heads = other.rearrange("(a p k) j -> a p (k j)", a=HEADS, p=P, k=TOKEN_BLOCKS)
-    context_rows = context.rearrange("(p k) d -> p (k d)", p=P, k=TOKEN_BLOCKS)
+    context_parts = context.rearrange("(p c k) d -> c p (k d)", p=P, c=CONTEXT_PARTS, k=BLOCKS_IN_PART)
     out_rows = out.rearrange("(b p) j -> p b j", p=P)
 
     with (
@@ -33,15 +36,19 @@ def tile_remodel_kernel(tc, x, other, context, offs, out):
 
         other_tiles = {}
         windows = {}
+        context_tiles = [
+            held.tile([P, BLOCKS_IN_PART * FEATURES], BF16, name=f"context{c}") for c in range(CONTEXT_PARTS)
+        ]
         for k in range(TOKEN_BLOCKS):
+            if k == TOKEN_BLOCKS - 1:
+                nc.sync.dma_start(context_tiles[0][:], context_parts[0])
             for a in range(HEADS):
                 if k == 0:
                     other_tiles[a] = held.tile([P, TOKEN_BLOCKS * PAIRS], F32, name=f"other{a}")
                     nc.scalar.dma_start(other_tiles[a][:], other_heads[a])
                 windows[a, k] = held.tile([P, ENTITIES], F32, name=f"window{a}_{k}")
                 nc.sync.dma_start(windows[a, k][:], x_blocks[a, k])
-        context_tile = held.tile([P, TOKEN_BLOCKS * FEATURES], BF16, name="context_tile")
-        nc.sync.dma_start(context_tile[:], context_rows)
+        nc.sync.dma_start(context_tiles[1][:], context_parts[1])
 
         ones = held.tile([P, P], BF16, name="ones")
         nc.gpsimd.memset(ones[:], 1.0)
@@ -52,8 +59,10 @@ def tile_remodel_kernel(tc, x, other, context, offs, out):
         nc.gpsimd.memset(eps_share[:], EPS / P)
         denominator = psum.tile([P, PAIRS], F32, name="denominator")
         nc.tensor.matmul(denominator[:], ones_f32[:], eps_share[:], start=True, stop=False)
-        q_blocks = []
+
+        numerators = [psum.tile([P, PAIRS], F32, name=f"numerator{b}") for b in range(FEATURE_BLOCKS)]
         for k in range(TOKEN_BLOCKS):
+            first, last = k == 0, k == TOKEN_BLOCKS - 1
             products = []
             for a in range(HEADS):
                 product = held.tile([P, PAIRS], F32, name=f"product{a}_{k}")
@@ -66,18 +75,15 @@ def tile_remodel_kernel(tc, x, other, context, offs, out):
                 products.append(product)
             q = held.tile([P, PAIRS], BF16, name=f"q{k}")
             nc.vector.tensor_tensor(q[:], products[0][:], products[1][:], ADD)
-            nc.tensor.matmul(denominator[:], ones[:], q[:], start=False, stop=k == TOKEN_BLOCKS - 1)
-            q_blocks.append(q)
+            nc.tensor.matmul(denominator[:], ones[:], q[:], start=False, stop=last)
+            block_features = context_tiles[k // BLOCKS_IN_PART][:, (k % BLOCKS_IN_PART) * FEATURES :]
+            for b in range(FEATURE_BLOCKS):
+                nc.tensor.matmul(numerators[b][:], block_features[:, b * P : (b + 1) * P], q[:], start=first, stop=last)
 
         inverse = held.tile([P, PAIRS], F32, name="inverse")
         nc.vector.reciprocal(inverse[:], denominator[:])
 
-        numerators = psum.tile([P, FEATURE_BLOCKS, PAIRS], F32, name="numerators")
-        for b in range(FEATURE_BLOCKS):
-            for k in range(TOKEN_BLOCKS):
-                features = context_tile[:, k * FEATURES + b * P : k * FEATURES + (b + 1) * P]
-                nc.tensor.matmul(numerators[:, b, :], features, q_blocks[k][:], start=k == 0, stop=k == TOKEN_BLOCKS - 1)
         pooled = held.tile([P, FEATURE_BLOCKS, PAIRS], F32, name="pooled")
-        inverse_for_each_block = inverse[:].unsqueeze(1).to_broadcast([P, FEATURE_BLOCKS, PAIRS])
-        nc.vector.tensor_tensor(pooled[:], numerators[:], inverse_for_each_block, MULT)
+        for b in range(FEATURE_BLOCKS):
+            nc.vector.tensor_tensor(pooled[:, b, :], numerators[b][:], inverse[:], MULT)
         nc.sync.dma_start(out_rows, pooled[:])

@@ -40,15 +40,14 @@ def tile_remodel_kernel(tc, x, other, context, offs, out):
             held.tile([P, BLOCKS_IN_PART * FEATURES], BF16, name=f"context{c}") for c in range(CONTEXT_PARTS)
         ]
         for k in range(TOKEN_BLOCKS):
-            if k == TOKEN_BLOCKS - 1:
-                nc.sync.dma_start(context_tiles[0][:], context_parts[0])
             for a in range(HEADS):
                 if k == 0:
                     other_tiles[a] = held.tile([P, TOKEN_BLOCKS * PAIRS], F32, name=f"other{a}")
                     nc.scalar.dma_start(other_tiles[a][:], other_heads[a])
                 windows[a, k] = held.tile([P, ENTITIES], F32, name=f"window{a}_{k}")
                 nc.sync.dma_start(windows[a, k][:], x_blocks[a, k])
-        nc.sync.dma_start(context_tiles[1][:], context_parts[1])
+        for c in range(CONTEXT_PARTS):
+            nc.sync.dma_start(context_tiles[c][:], context_parts[c])
 
         ones = held.tile([P, P], BF16, name="ones")
         nc.gpsimd.memset(ones[:], 1.0)

@@ -60,24 +60,30 @@ def tile_remodel_kernel(tc, x, other, context, offs, out):
         nc.tensor.matmul(denominator[:], ones_f32[:], eps_share[:], start=True, stop=False)
 
         numerators = [psum.tile([P, PAIRS], F32, name=f"numerator{b}") for b in range(FEATURE_BLOCKS)]
-        for k in range(TOKEN_BLOCKS):
-            first, last = k == 0, k == TOKEN_BLOCKS - 1
-            products = []
-            for a in range(HEADS):
-                product = held.tile([P, PAIRS], F32, name=f"product{a}_{k}")
-                nc.vector.tensor_tensor(
-                    product[:],
-                    windows[a, k][:].indirect(offsets[:]),
-                    other_tiles[a][:, k * PAIRS : (k + 1) * PAIRS],
-                    MULT,
-                )
-                products.append(product)
-            q = held.tile([P, PAIRS], BF16, name=f"q{k}")
+
+        for c in range(CONTEXT_PARTS):
+            products = [held.tile([P, BLOCKS_IN_PART * PAIRS], F32, name=f"products{a}_{c}") for a in range(HEADS)]
+            for i in range(BLOCKS_IN_PART):
+                k = c * BLOCKS_IN_PART + i
+                for a in range(HEADS):
+                    nc.vector.tensor_tensor(
+                        products[a][:, i * PAIRS : (i + 1) * PAIRS],
+                        windows[a, k][:].indirect(offsets[:]),
+                        other_tiles[a][:, k * PAIRS : (k + 1) * PAIRS],
+                        MULT,
+                    )
+            q = held.tile([P, BLOCKS_IN_PART * PAIRS], BF16, name=f"q{c}")
             nc.vector.tensor_tensor(q[:], products[0][:], products[1][:], ADD)
-            nc.tensor.matmul(denominator[:], ones[:], q[:], start=False, stop=last)
-            block_features = context_tiles[k // BLOCKS_IN_PART][:, (k % BLOCKS_IN_PART) * FEATURES :]
-            for b in range(FEATURE_BLOCKS):
-                nc.tensor.matmul(numerators[b][:], block_features[:, b * P : (b + 1) * P], q[:], start=first, stop=last)
+            for i in range(BLOCKS_IN_PART):
+                k = c * BLOCKS_IN_PART + i
+                q_block = q[:, i * PAIRS : (i + 1) * PAIRS]
+                nc.tensor.matmul(denominator[:], ones[:], q_block, start=False, stop=k == TOKEN_BLOCKS - 1)
+            for i in range(BLOCKS_IN_PART):
+                k = c * BLOCKS_IN_PART + i
+                q_block = q[:, i * PAIRS : (i + 1) * PAIRS]
+                for b in range(FEATURE_BLOCKS):
+                    features = context_tiles[c][:, i * FEATURES + b * P : i * FEATURES + (b + 1) * P]
+                    nc.tensor.matmul(numerators[b][:], features, q_block, start=k == 0, stop=k == TOKEN_BLOCKS - 1)
 
         inverse = held.tile([P, PAIRS], F32, name="inverse")
         nc.vector.reciprocal(inverse[:], denominator[:])

@@ -49,11 +49,9 @@ def tile_remodel_kernel(tc, x, other, context, offs, out):
         for c in range(CONTEXT_PARTS):
             nc.sync.dma_start(context_tiles[c][:], context_parts[c])
 
-        ones = held.tile([P, P], BF16, name="ones")
-        nc.gpsimd.memset(ones[:], 1.0)
-
         ones_f32 = held.tile([P, P], F32, name="ones_f32")
         nc.gpsimd.memset(ones_f32[:], 1.0)
+
         eps_share = held.tile([P, PAIRS], F32, name="eps_share")
         nc.gpsimd.memset(eps_share[:], EPS / P)
         denominator = psum.tile([P, PAIRS], F32, name="denominator")
@@ -66,18 +64,17 @@ def tile_remodel_kernel(tc, x, other, context, offs, out):
             for i in range(BLOCKS_IN_PART):
                 k = c * BLOCKS_IN_PART + i
                 for a in range(HEADS):
+                    product = products[a][:, i * PAIRS : (i + 1) * PAIRS]
                     nc.vector.tensor_tensor(
-                        products[a][:, i * PAIRS : (i + 1) * PAIRS],
+                        product,
                         windows[a, k][:].indirect(offsets[:]),
                         other_tiles[a][:, k * PAIRS : (k + 1) * PAIRS],
                         MULT,
                     )
+                    last_product = k == TOKEN_BLOCKS - 1 and a == HEADS - 1
+                    nc.tensor.matmul(denominator[:], ones_f32[:], product, start=False, stop=last_product)
             q = held.tile([P, BLOCKS_IN_PART * PAIRS], BF16, name=f"q{c}")
             nc.vector.tensor_tensor(q[:], products[0][:], products[1][:], ADD)
-            for i in range(BLOCKS_IN_PART):
-                k = c * BLOCKS_IN_PART + i
-                q_block = q[:, i * PAIRS : (i + 1) * PAIRS]
-                nc.tensor.matmul(denominator[:], ones[:], q_block, start=False, stop=k == TOKEN_BLOCKS - 1)
             for i in range(BLOCKS_IN_PART):
                 k = c * BLOCKS_IN_PART + i
                 q_block = q[:, i * PAIRS : (i + 1) * PAIRS]

@@ -32,7 +32,6 @@ def tile_remodel_kernel(tc, x, other, context, offs, out):
         tc.psum_pool(name="psum", bufs=1) as psum,
     ):
         offsets = held.tile([P, PAIRS // 16], U16, name="offsets")
-        nc.sync.dma_start(offsets[:], offs)
 
         other_tiles = {}
         windows = {}
@@ -43,9 +42,11 @@ def tile_remodel_kernel(tc, x, other, context, offs, out):
             for a in range(HEADS):
                 if k == 0:
                     other_tiles[a] = held.tile([P, TOKEN_BLOCKS * PAIRS], F32, name=f"other{a}")
-                    nc.scalar.dma_start(other_tiles[a][:], other_heads[a])
+                    nc.sync.dma_start(other_tiles[a][:], other_heads[a])
                 windows[a, k] = held.tile([P, ENTITIES], F32, name=f"window{a}_{k}")
                 nc.sync.dma_start(windows[a, k][:], x_blocks[a, k])
+                if k == 0 and a == 0:
+                    nc.sync.dma_start(offsets[:], offs)
         for c in range(CONTEXT_PARTS):
             nc.sync.dma_start(context_tiles[c][:], context_parts[c])
 

@@ -58,7 +58,8 @@ def tile_remodel_kernel(tc, x, other, context, offs, out):
         denominator = psum.tile([P, PAIRS], F32, name="denominator")
         nc.tensor.matmul(denominator[:], ones_f32[:], eps_share[:], start=True, stop=False)
 
-        numerators = [psum.tile([P, PAIRS], F32, name=f"numerator{b}") for b in range(FEATURE_BLOCKS)]
+        numerators = psum.tile([P, FEATURE_BLOCKS, PAIRS], F32, name="numerators")
+        q_parts = []
 
         for c in range(CONTEXT_PARTS):
             products = [held.tile([P, BLOCKS_IN_PART * PAIRS], F32, name=f"products{a}_{c}") for a in range(HEADS)]
@@ -76,17 +77,19 @@ def tile_remodel_kernel(tc, x, other, context, offs, out):
                     nc.tensor.matmul(denominator[:], ones_f32[:], product, start=False, stop=last_product)
             q = held.tile([P, BLOCKS_IN_PART * PAIRS], BF16, name=f"q{c}")
             nc.vector.tensor_tensor(q[:], products[0][:], products[1][:], ADD)
-            for i in range(BLOCKS_IN_PART):
-                k = c * BLOCKS_IN_PART + i
-                q_block = q[:, i * PAIRS : (i + 1) * PAIRS]
-                for b in range(FEATURE_BLOCKS):
-                    features = context_tiles[c][:, i * FEATURES + b * P : i * FEATURES + (b + 1) * P]
-                    nc.tensor.matmul(numerators[b][:], features, q_block, start=k == 0, stop=k == TOKEN_BLOCKS - 1)
+            q_parts.append(q)
+
+        for b in range(FEATURE_BLOCKS):
+            for k in range(TOKEN_BLOCKS):
+                c, i = divmod(k, BLOCKS_IN_PART)
+                features = context_tiles[c][:, i * FEATURES + b * P : i * FEATURES + (b + 1) * P]
+                q_block = q_parts[c][:, i * PAIRS : (i + 1) * PAIRS]
+                nc.tensor.matmul(numerators[:, b, :], features, q_block, start=k == 0, stop=k == TOKEN_BLOCKS - 1)
 
         inverse = held.tile([P, PAIRS], F32, name="inverse")
         nc.vector.reciprocal(inverse[:], denominator[:])
 
         pooled = held.tile([P, FEATURE_BLOCKS, PAIRS], F32, name="pooled")
-        for b in range(FEATURE_BLOCKS):
-            nc.vector.tensor_tensor(pooled[:, b, :], numerators[b][:], inverse[:], MULT)
+        inverse_for_each_block = inverse[:].unsqueeze(1).to_broadcast([P, FEATURE_BLOCKS, PAIRS])
+        nc.vector.tensor_tensor(pooled[:], numerators[:], inverse_for_each_block, MULT)
         nc.sync.dma_start(out_rows, pooled[:])

@@ -17,6 +17,7 @@ FLOPS = 2 * HEADS * TOKENS * PAIRS + 2 * TOKENS * PAIRS * (FEATURES + 1)
 
 CONTEXT_PARTS = 2
 BLOCKS_IN_PART = TOKEN_BLOCKS // CONTEXT_PARTS
+PAIR_PARTS = [(0, 3 * PAIRS // 4), (3 * PAIRS // 4, PAIRS)]
 
 
 def tile_remodel_kernel(tc, x, other, context, offs, out):
@@ -86,10 +87,13 @@ def tile_remodel_kernel(tc, x, other, context, offs, out):
                 q_block = q_parts[c][:, i * PAIRS : (i + 1) * PAIRS]
                 nc.tensor.matmul(numerators[:, b, :], features, q_block, start=k == 0, stop=k == TOKEN_BLOCKS - 1)
 
-        inverse = held.tile([P, PAIRS], F32, name="inverse")
-        nc.vector.reciprocal(inverse[:], denominator[:])
-
         pooled = held.tile([P, FEATURE_BLOCKS, PAIRS], F32, name="pooled")
-        inverse_for_each_block = inverse[:].unsqueeze(1).to_broadcast([P, FEATURE_BLOCKS, PAIRS])
-        nc.vector.tensor_tensor(pooled[:], numerators[:], inverse_for_each_block, MULT)
+        inverses = []
+        for start, end in PAIR_PARTS:
+            inverse = held.tile([P, end - start], F32, name=f"inverse{start}")
+            nc.vector.reciprocal(inverse[:], denominator[:, start:end])
+            inverses.append(inverse)
+        for (start, end), inverse in zip(PAIR_PARTS, inverses):
+            inverse_for_each_block = inverse[:].unsqueeze(1).to_broadcast([P, FEATURE_BLOCKS, end - start])
+            nc.vector.tensor_tensor(pooled[:, :, start:end], numerators[:, :, start:end], inverse_for_each_block, MULT)
         nc.sync.dma_start(out_rows, pooled[:])

@@ -39,15 +39,16 @@ def tile_remodel_kernel(tc, x, other, context, offs, out):
         context_tiles = [
             held.tile([P, BLOCKS_IN_PART * FEATURES], BF16, name=f"context{c}") for c in range(CONTEXT_PARTS)
         ]
-        for k in range(TOKEN_BLOCKS):
+        for c in range(CONTEXT_PARTS):
             for a in range(HEADS):
-                if k == 0:
+                if c == 0:
                     other_tiles[a] = held.tile([P, TOKEN_BLOCKS * PAIRS], F32, name=f"other{a}")
                     nc.sync.dma_start(other_tiles[a][:], other_heads[a])
-                windows[a, k] = held.tile([P, ENTITIES], F32, name=f"window{a}_{k}")
-                nc.sync.dma_start(windows[a, k][:], x_blocks[a, k])
-                if k == 0 and a == 0:
-                    nc.sync.dma_start(offsets[:], offs)
+                for k in range(c * BLOCKS_IN_PART, (c + 1) * BLOCKS_IN_PART):
+                    windows[a, k] = held.tile([P, ENTITIES], F32, name=f"window{a}_{k}")
+                    nc.sync.dma_start(windows[a, k][:], x_blocks[a, k])
+                    if a == 0 and k == 0:
+                        nc.sync.dma_start(offsets[:], offs)
         for c in range(CONTEXT_PARTS):
             nc.sync.dma_start(context_tiles[c][:], context_parts[c])
 
@@ -64,9 +65,9 @@ def tile_remodel_kernel(tc, x, other, context, offs, out):
 
         for c in range(CONTEXT_PARTS):
             products = [held.tile([P, BLOCKS_IN_PART * PAIRS], F32, name=f"products{a}_{c}") for a in range(HEADS)]
-            for i in range(BLOCKS_IN_PART):
-                k = c * BLOCKS_IN_PART + i
-                for a in range(HEADS):
+            for a in range(HEADS):
+                for i in range(BLOCKS_IN_PART):
+                    k = c * BLOCKS_IN_PART + i
                     product = products[a][:, i * PAIRS : (i + 1) * PAIRS]
                     nc.vector.tensor_tensor(
                         product,

@@ -26,7 +26,7 @@ def tile_remodel_kernel(tc, x, other, context, offs, out):
     x_blocks = x.rearrange("(a p k) s -> a k p s", a=HEADS, p=P, k=TOKEN_BLOCKS)
     other_heads = other.rearrange("(a p k) j -> a p (k j)", a=HEADS, p=P, k=TOKEN_BLOCKS)
     context_parts = context.rearrange("(p c k) d -> c p (k d)", p=P, c=CONTEXT_PARTS, k=BLOCKS_IN_PART)
-    out_rows = out.rearrange("(b p) j -> p b j", p=P)
+    out_rows = out.rearrange("(p b) j -> p b j", p=P)
 
     with (
         tc.tile_pool(name="held", bufs=1) as held,
@@ -84,7 +84,7 @@ def tile_remodel_kernel(tc, x, other, context, offs, out):
         for b in range(FEATURE_BLOCKS):
             for k in range(TOKEN_BLOCKS):
                 c, i = divmod(k, BLOCKS_IN_PART)
-                features = context_tiles[c][:, i * FEATURES + b * P : i * FEATURES + (b + 1) * P]
+                features = context_tiles[c][:, i * FEATURES + b : (i + 1) * FEATURES : FEATURE_BLOCKS]
                 q_block = q_parts[c][:, i * PAIRS : (i + 1) * PAIRS]
                 nc.tensor.matmul(numerators[:, b, :], features, q_block, start=k == 0, stop=k == TOKEN_BLOCKS - 1)
 

import concourse.mybir as mybir

F32, BF16, U16 = mybir.dt.float32, mybir.dt.bfloat16, mybir.dt.uint16
MULT, ADD = mybir.AluOpType.mult, mybir.AluOpType.add

P = 128
HEADS = 2
TOKENS = 512
ENTITIES = 384
PAIRS = 128
FEATURES = 256
TOKEN_BLOCKS = TOKENS // P
FEATURE_BLOCKS = FEATURES // P
EPS = 2.0**-14 * (1.0 + 2.0**-14) ** 2

FLOPS = 2 * HEADS * TOKENS * PAIRS + 2 * TOKENS * PAIRS * (FEATURES + 1)

CONTEXT_PARTS = 2
BLOCKS_IN_PART = TOKEN_BLOCKS // CONTEXT_PARTS
PAIR_PARTS = [(0, 3 * PAIRS // 4), (3 * PAIRS // 4, PAIRS)]


def tile_remodel_kernel(tc, x, other, context, offs, out):
    nc = tc.nc

    x_blocks = x.rearrange("(a p k) s -> a k p s", a=HEADS, p=P, k=TOKEN_BLOCKS)
    other_heads = other.rearrange("(a p k) j -> a p (k j)", a=HEADS, p=P, k=TOKEN_BLOCKS)
    context_parts = context.rearrange("(p c k) d -> c p (k d)", p=P, c=CONTEXT_PARTS, k=BLOCKS_IN_PART)
    out_rows = out.rearrange("(p b) j -> p b j", p=P)

    with (
        tc.tile_pool(name="held", bufs=1) as held,
        tc.psum_pool(name="psum", bufs=1) as psum,
    ):
        offsets = held.tile([P, PAIRS // 16], U16, name="offsets")

        other_tiles = {}
        windows = {}
        context_tiles = [
            held.tile([P, BLOCKS_IN_PART * FEATURES], BF16, name=f"context{c}") for c in range(CONTEXT_PARTS)
        ]
        for c in range(CONTEXT_PARTS):
            for a in range(HEADS):
                if c == 0:
                    other_tiles[a] = held.tile([P, TOKEN_BLOCKS * PAIRS], F32, name=f"other{a}")
                    nc.sync.dma_start(other_tiles[a][:], other_heads[a])
                for k in range(c * BLOCKS_IN_PART, (c + 1) * BLOCKS_IN_PART):
                    windows[a, k] = held.tile([P, ENTITIES], F32, name=f"window{a}_{k}")
                    nc.sync.dma_start(windows[a, k][:], x_blocks[a, k])
                    if a == 0 and k == 0:
                        nc.sync.dma_start(offsets[:], offs)
        for c in range(CONTEXT_PARTS):
            nc.sync.dma_start(context_tiles[c][:], context_parts[c])

        ones_f32 = held.tile([P, P], F32, name="ones_f32")
        nc.gpsimd.memset(ones_f32[:], 1.0)

        eps_share = held.tile([P, PAIRS], F32, name="eps_share")
        nc.gpsimd.memset(eps_share[:], EPS / P)
        denominator = psum.tile([P, PAIRS], F32, name="denominator")
        nc.tensor.matmul(denominator[:], ones_f32[:], eps_share[:], start=True, stop=False)

        numerators = psum.tile([P, FEATURE_BLOCKS, PAIRS], F32, name="numerators")
        q_parts = []

        for c in range(CONTEXT_PARTS):
            products = [held.tile([P, BLOCKS_IN_PART * PAIRS], F32, name=f"products{a}_{c}") for a in range(HEADS)]
            for a in range(HEADS):
                for i in range(BLOCKS_IN_PART):
                    k = c * BLOCKS_IN_PART + i
                    product = products[a][:, i * PAIRS : (i + 1) * PAIRS]
                    nc.vector.tensor_tensor(
                        product,
                        windows[a, k][:].indirect(offsets[:]),
                        other_tiles[a][:, k * PAIRS : (k + 1) * PAIRS],
                        MULT,
                    )
                    last_product = k == TOKEN_BLOCKS - 1 and a == HEADS - 1
                    nc.tensor.matmul(denominator[:], ones_f32[:], product, start=False, stop=last_product)
            q = held.tile([P, BLOCKS_IN_PART * PAIRS], BF16, name=f"q{c}")
            nc.vector.tensor_tensor(q[:], products[0][:], products[1][:], ADD)
            q_parts.append(q)

        for b in range(FEATURE_BLOCKS):
            for k in range(TOKEN_BLOCKS):
                c, i = divmod(k, BLOCKS_IN_PART)
                features = context_tiles[c][:, i * FEATURES + b : (i + 1) * FEATURES : FEATURE_BLOCKS]
                q_block = q_parts[c][:, i * PAIRS : (i + 1) * PAIRS]
                nc.tensor.matmul(numerators[:, b, :], features, q_block, start=k == 0, stop=k == TOKEN_BLOCKS - 1)

        pooled = held.tile([P, FEATURE_BLOCKS, PAIRS], F32, name="pooled")
        inverses = []
        for start, end in PAIR_PARTS:
            inverse = held.tile([P, end - start], F32, name=f"inverse{start}")
            nc.vector.reciprocal(inverse[:], denominator[:, start:end])
            inverses.append(inverse)
        for (start, end), inverse in zip(PAIR_PARTS, inverses):
            inverse_for_each_block = inverse[:].unsqueeze(1).to_broadcast([P, FEATURE_BLOCKS, end - start])
            nc.vector.tensor_tensor(pooled[:, :, start:end], numerators[:, :, start:end], inverse_for_each_block, MULT)
        nc.sync.dma_start(out_rows, pooled[:])
